import numpy as np
import ml_dtypes

BF16 = ml_dtypes.bfloat16


def bf(x):
    return np.asarray(x, np.float32).astype(BF16)


def f32(x):
    return np.asarray(x, np.float32)


def f64(x):
    return np.asarray(x).astype(np.float64)


def striped(idx):
    return np.tile(idx.reshape(-1, 16).T, (8, 1))


F, H, M, S, N = 128, 128, 128, 1024, 128
XAV = np.sqrt(6.0 / (F + H))
XAV_M = np.sqrt(6.0 / (H + M))


def setup_inputs():
    return {"table": bf(np.random.standard_normal((F, S))), "w": bf(np.random.uniform(-XAV, XAV, (F, H))), "gene_a": bf(np.random.standard_normal((F, N))), "gene_b": f32(np.random.standard_normal((H, N))), "drug": f32(np.random.standard_normal((H, N))), "w_dis": bf(np.random.uniform(-XAV_M, XAV_M, (H, M))), "offs": striped(np.random.permutation(np.tile(np.arange(S), 2))[:N])}


def reference(table, w, gene_a, gene_b, drug, w_dis, offs):
    idx = offs[:16].T.reshape(-1)
    t = f64(w).T @ f64(table)[:, idx] + f64(w).T @ f64(gene_a)
    d = ((0.5 * t + f64(gene_b)) * 0.5 + f64(drug)) * 0.5
    return f64(w_dis).T @ d

@@ -1,0 +1,51 @@
+import concourse.mybir as mybir
+
+F = 128
+H = 128
+M = 128
+S = 1024
+N = 128
+
+FLOPS = 2 * F * H * N * 2 + 2 * H * M * N
+
+BF16, F32, U16 = mybir.dt.bfloat16, mybir.dt.float32, mybir.dt.uint16
+MULT, ADD = mybir.AluOpType.mult, mybir.AluOpType.add
+
+
+def tile_metapathaggregator_kernel(tc, table, w, gene_a, gene_b, drug, w_dis, offs, out):
+    nc = tc.nc
+    with (
+        tc.tile_pool(name="held", bufs=1) as held,
+        tc.psum_pool(name="psum", bufs=1) as psum,
+    ):
+        offsets = held.tile([F, N // 16], U16, name="offsets")
+        table_sb = held.tile([F, S], BF16, name="table_sb")
+        w_sb = held.tile([F, H], BF16, name="w_sb")
+        gene_a_sb = held.tile([F, N], BF16, name="gene_a_sb")
+        gene_b_sb = held.tile([H, N], F32, name="gene_b_sb")
+        drug_sb = held.tile([H, N], F32, name="drug_sb")
+        w_dis_sb = held.tile([H, M], BF16, name="w_dis_sb")
+
+        nc.sync.dma_start(offsets[:], offs)
+        nc.scalar.dma_start(w_sb[:], w)
+        nc.sync.dma_start(table_sb[:], table)
+        nc.scalar.dma_start(gene_a_sb[:], gene_a)
+        nc.sync.dma_start(gene_b_sb[:], gene_b)
+        nc.scalar.dma_start(drug_sb[:], drug)
+        nc.scalar.dma_start(w_dis_sb[:], w_dis)
+
+        t_ps = psum.tile([H, N], F32, name="t_ps")
+        nc.tensor.matmul(t_ps[:], w_sb[:], gene_a_sb[:], start=True, stop=False)
+        nc.tensor.matmul(t_ps[:], w_sb[:], table_sb[:].indirect(offsets[:]), start=False, stop=True)
+
+        rest = held.tile([H, N], F32, name="rest")
+        nc.vector.tensor_scalar_mul(rest[:], drug_sb[:], 0.5)
+        nc.vector.scalar_tensor_tensor(rest[:], gene_b_sb[:], 0.25, rest[:], MULT, ADD)
+        d_bf = held.tile([H, N], BF16, name="d_bf")
+        nc.vector.scalar_tensor_tensor(d_bf[:], t_ps[:], 0.125, rest[:], MULT, ADD)
+
+        out_ps = psum.tile([M, N], F32, name="out_ps")
+        nc.tensor.matmul(out_ps[:], w_dis_sb[:], d_bf[:], start=True, stop=True)
+        out_sb = held.tile([M, N], F32, name="out_sb")
+        nc.vector.tensor_copy(out_sb[:], out_ps[:])
+        nc.sync.dma_start(out, out_sb[:])

@@ -27,12 +27,12 @@ def tile_metapathaggregator_kernel(tc, table, w, gene_a, gene_b, drug, w_dis, of
         w_dis_sb = held.tile([H, M], BF16, name="w_dis_sb")
 
         nc.sync.dma_start(offsets[:], offs)
-        nc.scalar.dma_start(w_sb[:], w)
+        nc.sync.dma_start(w_sb[:], w)
+        nc.sync.dma_start(gene_a_sb[:], gene_a)
         nc.sync.dma_start(table_sb[:], table)
-        nc.scalar.dma_start(gene_a_sb[:], gene_a)
+        nc.sync.dma_start(drug_sb[:], drug)
         nc.sync.dma_start(gene_b_sb[:], gene_b)
-        nc.scalar.dma_start(drug_sb[:], drug)
-        nc.scalar.dma_start(w_dis_sb[:], w_dis)
+        nc.sync.dma_start(w_dis_sb[:], w_dis)
 
         t_ps = psum.tile([H, N], F32, name="t_ps")
         nc.tensor.matmul(t_ps[:], w_sb[:], gene_a_sb[:], start=True, stop=False)

@@ -5,6 +5,8 @@ H = 128
 M = 128
 S = 1024
 N = 128
+HALF = N // 2
+BANK = 512
 
 FLOPS = 2 * F * H * N * 2 + 2 * H * M * N
 
@@ -41,11 +43,15 @@ def tile_metapathaggregator_kernel(tc, table, w, gene_a, gene_b, drug, w_dis, of
         rest = held.tile([H, N], F32, name="rest")
         nc.vector.tensor_scalar_mul(rest[:], drug_sb[:], 0.5)
         nc.vector.scalar_tensor_tensor(rest[:], gene_b_sb[:], 0.25, rest[:], MULT, ADD)
+        halves = [slice(k * HALF, (k + 1) * HALF) for k in range(N // HALF)]
         d_bf = held.tile([H, N], BF16, name="d_bf")
-        nc.vector.scalar_tensor_tensor(d_bf[:], t_ps[:], 0.125, rest[:], MULT, ADD)
+        for cols in halves:
+            nc.vector.scalar_tensor_tensor(d_bf[:, cols], t_ps[:, cols], 0.125, rest[:, cols], MULT, ADD)
 
-        out_ps = psum.tile([M, N], F32, name="out_ps")
-        nc.tensor.matmul(out_ps[:], w_dis_sb[:], d_bf[:], start=True, stop=True)
+        out_ps = [psum.tile([M, BANK], F32, name="out_ps%d" % k) for k in range(len(halves))]
+        for k, cols in enumerate(halves):
+            nc.tensor.matmul(out_ps[k][:, :HALF], w_dis_sb[:], d_bf[:, cols], start=True, stop=True)
         out_sb = held.tile([M, N], F32, name="out_sb")
-        nc.vector.tensor_copy(out_sb[:], out_ps[:])
+        for k, cols in enumerate(halves):
+            nc.vector.tensor_copy(out_sb[:, cols], out_ps[k][:, :HALF])
         nc.sync.dma_start(out, out_sb[:])

@@ -28,24 +28,24 @@ def tile_metapathaggregator_kernel(tc, table, w, gene_a, gene_b, drug, w_dis, of
         drug_sb = held.tile([H, N], F32, name="drug_sb")
         w_dis_sb = held.tile([H, M], BF16, name="w_dis_sb")
 
+        nc.sync.dma_start(table_sb[:], table)
         nc.sync.dma_start(offsets[:], offs)
         nc.sync.dma_start(w_sb[:], w)
         nc.sync.dma_start(gene_a_sb[:], gene_a)
-        nc.sync.dma_start(table_sb[:], table)
         nc.sync.dma_start(drug_sb[:], drug)
         nc.sync.dma_start(gene_b_sb[:], gene_b)
         nc.sync.dma_start(w_dis_sb[:], w_dis)
 
         t_ps = psum.tile([H, N], F32, name="t_ps")
-        nc.tensor.matmul(t_ps[:], w_sb[:], gene_a_sb[:], start=True, stop=False)
-        nc.tensor.matmul(t_ps[:], w_sb[:], table_sb[:].indirect(offsets[:]), start=False, stop=True)
+        nc.tensor.matmul(t_ps[:], w_sb[:], table_sb[:].indirect(offsets[:]), start=True, stop=False)
+        nc.tensor.matmul(t_ps[:], w_sb[:], gene_a_sb[:], start=False, stop=True)
 
         rest = held.tile([H, N], F32, name="rest")
         nc.vector.tensor_scalar_mul(rest[:], drug_sb[:], 0.5)
-        nc.vector.scalar_tensor_tensor(rest[:], gene_b_sb[:], 0.25, rest[:], MULT, ADD)
         halves = [slice(k * HALF, (k + 1) * HALF) for k in range(N // HALF)]
         d_bf = held.tile([H, N], BF16, name="d_bf")
         for cols in halves:
+            nc.vector.scalar_tensor_tensor(rest[:, cols], gene_b_sb[:, cols], 0.25, rest[:, cols], MULT, ADD)
             nc.vector.scalar_tensor_tensor(d_bf[:, cols], t_ps[:, cols], 0.125, rest[:, cols], MULT, ADD)
 
         out_ps = [psum.tile([M, BANK], F32, name="out_ps%d" % k) for k in range(len(halves))]

@@ -31,9 +31,9 @@ def tile_metapathaggregator_kernel(tc, table, w, gene_a, gene_b, drug, w_dis, of
         nc.sync.dma_start(table_sb[:], table)
         nc.sync.dma_start(offsets[:], offs)
         nc.sync.dma_start(w_sb[:], w)
-        nc.sync.dma_start(gene_a_sb[:], gene_a)
         nc.sync.dma_start(drug_sb[:], drug)
         nc.sync.dma_start(gene_b_sb[:], gene_b)
+        nc.sync.dma_start(gene_a_sb[:], gene_a)
         nc.sync.dma_start(w_dis_sb[:], w_dis)
 
         t_ps = psum.tile([H, N], F32, name="t_ps")

@@ -40,18 +40,17 @@ def tile_metapathaggregator_kernel(tc, table, w, gene_a, gene_b, drug, w_dis, of
         nc.tensor.matmul(t_ps[:], w_sb[:], table_sb[:].indirect(offsets[:]), start=True, stop=False)
         nc.tensor.matmul(t_ps[:], w_sb[:], gene_a_sb[:], start=False, stop=True)
 
-        rest = held.tile([H, N], F32, name="rest")
-        nc.vector.tensor_scalar_mul(rest[:], drug_sb[:], 0.5)
         halves = [slice(k * HALF, (k + 1) * HALF) for k in range(N // HALF)]
-        d_bf = held.tile([H, N], BF16, name="d_bf")
+        twice_rest = held.tile([H, N], F32, name="twice_rest")
+        twice_d_bf = held.tile([H, N], BF16, name="twice_d_bf")
         for cols in halves:
-            nc.vector.scalar_tensor_tensor(rest[:, cols], gene_b_sb[:, cols], 0.25, rest[:, cols], MULT, ADD)
-            nc.vector.scalar_tensor_tensor(d_bf[:, cols], t_ps[:, cols], 0.125, rest[:, cols], MULT, ADD)
+            nc.vector.scalar_tensor_tensor(twice_rest[:, cols], gene_b_sb[:, cols], 0.5, drug_sb[:, cols], MULT, ADD)
+            nc.vector.scalar_tensor_tensor(twice_d_bf[:, cols], t_ps[:, cols], 0.25, twice_rest[:, cols], MULT, ADD)
 
         out_ps = [psum.tile([M, BANK], F32, name="out_ps%d" % k) for k in range(len(halves))]
         for k, cols in enumerate(halves):
-            nc.tensor.matmul(out_ps[k][:, :HALF], w_dis_sb[:], d_bf[:, cols], start=True, stop=True)
+            nc.tensor.matmul(out_ps[k][:, :HALF], w_dis_sb[:], twice_d_bf[:, cols], start=True, stop=True)
         out_sb = held.tile([M, N], F32, name="out_sb")
         for k, cols in enumerate(halves):
-            nc.vector.tensor_copy(out_sb[:, cols], out_ps[k][:, :HALF])
+            nc.vector.tensor_scalar_mul(out_sb[:, cols], out_ps[k][:, :HALF], 0.5)
         nc.sync.dma_start(out, out_sb[:])

@@ -5,7 +5,7 @@ H = 128
 M = 128
 S = 1024
 N = 128
-HALF = N // 2
+QUARTER = N // 4
 BANK = 512
 
 FLOPS = 2 * F * H * N * 2 + 2 * H * M * N
@@ -40,17 +40,17 @@ def tile_metapathaggregator_kernel(tc, table, w, gene_a, gene_b, drug, w_dis, of
         nc.tensor.matmul(t_ps[:], w_sb[:], table_sb[:].indirect(offsets[:]), start=True, stop=False)
         nc.tensor.matmul(t_ps[:], w_sb[:], gene_a_sb[:], start=False, stop=True)
 
-        halves = [slice(k * HALF, (k + 1) * HALF) for k in range(N // HALF)]
+        quarters = [slice(k * QUARTER, (k + 1) * QUARTER) for k in range(N // QUARTER)]
         twice_rest = held.tile([H, N], F32, name="twice_rest")
         twice_d_bf = held.tile([H, N], BF16, name="twice_d_bf")
-        for cols in halves:
+        for cols in quarters:
             nc.vector.scalar_tensor_tensor(twice_rest[:, cols], gene_b_sb[:, cols], 0.5, drug_sb[:, cols], MULT, ADD)
             nc.vector.scalar_tensor_tensor(twice_d_bf[:, cols], t_ps[:, cols], 0.25, twice_rest[:, cols], MULT, ADD)
 
-        out_ps = [psum.tile([M, BANK], F32, name="out_ps%d" % k) for k in range(len(halves))]
-        for k, cols in enumerate(halves):
-            nc.tensor.matmul(out_ps[k][:, :HALF], w_dis_sb[:], twice_d_bf[:, cols], start=True, stop=True)
+        out_ps = [psum.tile([M, BANK], F32, name="out_ps%d" % k) for k in range(len(quarters))]
+        for k, cols in enumerate(quarters):
+            nc.tensor.matmul(out_ps[k][:, :QUARTER], w_dis_sb[:], twice_d_bf[:, cols], start=True, stop=True)
         out_sb = held.tile([M, N], F32, name="out_sb")
-        for k, cols in enumerate(halves):
-            nc.vector.tensor_scalar_mul(out_sb[:, cols], out_ps[k][:, :HALF], 0.5)
+        for k, cols in enumerate(quarters):
+            nc.vector.tensor_scalar_mul(out_sb[:, cols], out_ps[k][:, :QUARTER], 0.5)
         nc.sync.dma_start(out, out_sb[:])

import concourse.mybir as mybir

F = 128
H = 128
M = 128
S = 1024
N = 128
QUARTER = N // 4
BANK = 512

FLOPS = 2 * F * H * N * 2 + 2 * H * M * N

BF16, F32, U16 = mybir.dt.bfloat16, mybir.dt.float32, mybir.dt.uint16
MULT, ADD = mybir.AluOpType.mult, mybir.AluOpType.add


def tile_metapathaggregator_kernel(tc, table, w, gene_a, gene_b, drug, w_dis, offs, out):
    nc = tc.nc
    with (
        tc.tile_pool(name="held", bufs=1) as held,
        tc.psum_pool(name="psum", bufs=1) as psum,
    ):
        offsets = held.tile([F, N // 16], U16, name="offsets")
        table_sb = held.tile([F, S], BF16, name="table_sb")
        w_sb = held.tile([F, H], BF16, name="w_sb")
        gene_a_sb = held.tile([F, N], BF16, name="gene_a_sb")
        gene_b_sb = held.tile([H, N], F32, name="gene_b_sb")
        drug_sb = held.tile([H, N], F32, name="drug_sb")
        w_dis_sb = held.tile([H, M], BF16, name="w_dis_sb")

        nc.sync.dma_start(table_sb[:], table)
        nc.sync.dma_start(offsets[:], offs)
        nc.sync.dma_start(w_sb[:], w)
        nc.sync.dma_start(drug_sb[:], drug)
        nc.sync.dma_start(gene_b_sb[:], gene_b)
        nc.sync.dma_start(gene_a_sb[:], gene_a)
        nc.sync.dma_start(w_dis_sb[:], w_dis)

        t_ps = psum.tile([H, N], F32, name="t_ps")
        nc.tensor.matmul(t_ps[:], w_sb[:], table_sb[:].indirect(offsets[:]), start=True, stop=False)
        nc.tensor.matmul(t_ps[:], w_sb[:], gene_a_sb[:], start=False, stop=True)

        quarters = [slice(k * QUARTER, (k + 1) * QUARTER) for k in range(N // QUARTER)]
        twice_rest = held.tile([H, N], F32, name="twice_rest")
        twice_d_bf = held.tile([H, N], BF16, name="twice_d_bf")
        for cols in quarters:
            nc.vector.scalar_tensor_tensor(twice_rest[:, cols], gene_b_sb[:, cols], 0.5, drug_sb[:, cols], MULT, ADD)
            nc.vector.scalar_tensor_tensor(twice_d_bf[:, cols], t_ps[:, cols], 0.25, twice_rest[:, cols], MULT, ADD)

        out_ps = [psum.tile([M, BANK], F32, name="out_ps%d" % k) for k in range(len(quarters))]
        for k, cols in enumerate(quarters):
            nc.tensor.matmul(out_ps[k][:, :QUARTER], w_dis_sb[:], twice_d_bf[:, cols], start=True, stop=True)
        out_sb = held.tile([M, N], F32, name="out_sb")
        for k, cols in enumerate(quarters):
            nc.vector.tensor_scalar_mul(out_sb[:, cols], out_ps[k][:, :QUARTER], 0.5)
        nc.sync.dma_start(out, out_sb[:])
